import numpy as np
import ml_dtypes


def mxq(x, axis, fmt="e4m3"):
    dtype, down = {"e4m3": (ml_dtypes.float8_e4m3fn, 7), "e5m2": (ml_dtypes.float8_e5m2, 14)}[fmt]
    v = np.moveaxis(np.asarray(x, np.float32).astype(ml_dtypes.bfloat16).astype(np.float64), axis, -1)
    blocks = v.reshape(v.shape[:-1] + (-1, 32))
    amax = np.abs(blocks).max(-1, keepdims=True)
    byte = np.maximum(np.where(amax > 0, np.frexp(amax)[1] - 1 + 127, 0) - down, 1)
    scale = np.exp2(byte - 127.0)
    codes = (blocks / scale).astype(np.float32).astype(dtype).astype(np.float64)
    return np.moveaxis((codes * scale).reshape(v.shape), -1, axis)


WIDE = False


def mx_kscale(k):
    if not WIDE:
        return np.ones(k)
    levels = np.array([20, -20, 10, -10, 0])
    a = np.random.permutation(np.resize(levels, k // 512 * 4)).reshape(k // 512, 4)
    idx = np.arange(k)
    return np.exp2(a[idx // 512, idx % 128 // 32])


BF16 = ml_dtypes.bfloat16


def bf(x):
    return np.asarray(x, np.float32).astype(BF16)


def f64(x):
    return np.asarray(x).astype(np.float64)


N, CI, CO, H, W, KH, KW = 2, 8192, 256, 16, 16, 3, 2
HO, WO = H - KH + 1, W - KW + 1
L = N * HO * WO
K = KH * KW * CI


def setup_inputs():
    u = np.unique(mx_kscale(K))
    s = u[((np.arange(CI) // 32) * (len(u) - 1)) % len(u)][None, :, None, None]
    x = np.random.standard_normal((N, CI, H, W)) * s
    go = np.random.standard_normal((N, CO, HO, WO)) / np.sqrt(L)
    g = np.random.standard_normal((CO, CI, KH, KW)) * np.exp2(np.random.randint(-12, 1, (CO, 1, 1, 1))) * 0.25 / s
    return {"input": bf(x), "grad_output": bf(go), "grad_out": bf(g)}


def reference(input, grad_output, grad_out):
    xq = mxq(f64(input), 1, "e4m3")
    gq = mxq(f64(grad_out), 1, "e5m2")
    a = gq.transpose(0, 2, 3, 1).reshape(CO, K)
    wins = np.stack([xq[:, :, i:i + HO, j:j + WO] for i in range(KH) for j in range(KW)], axis=0)
    b = wins.transpose(0, 2, 1, 3, 4).reshape(K, L)
    y = a @ b
    return np.ascontiguousarray(y.reshape(CO, N, HO, WO).transpose(1, 0, 2, 3))

@@ -1,0 +1,198 @@
+from contextlib import ExitStack
+
+import concourse.mybir as mybir
+from concourse.masks import make_identity
+
+BF16 = mybir.dt.bfloat16
+F32 = mybir.dt.float32
+I32 = mybir.dt.int32
+U32 = mybir.dt.uint32
+U8 = mybir.dt.uint8
+E4M3_X4 = mybir.dt.float8_e4m3fn_x4
+E5M2_X4 = mybir.dt.float8_e5m2_x4
+
+IMAGES, CI, CO, H, W, KH, KW = 2, 8192, 256, 16, 16, 3, 2
+HO, WO = H - KH + 1, W - KW + 1
+
+P = 128
+PACK = 4
+K_PASS = P * PACK
+PASSES = CI // K_PASS
+O_TILES = CO // P
+PIXELS = IMAGES * H * W
+ROW_STEP = IMAGES * W
+PAD = (KH - 1) * ROW_STEP
+X_WIDTH = PIXELS + PAD
+
+UNITS = 4
+SCALAR_UNITS = 3
+AHEAD = 4
+
+FLOPS = 2 * CO * CI * KH * KW * IMAGES * HO * WO
+
+
+def tile_model_pa_k_kernel(tc, x, grad_output, g, out):
+    nc = tc.nc
+
+    x_view = x.rearrange("n (s p j) h w -> s p n (j h w)", p=P, j=PACK)
+    g_view = g.rearrange("(t o) (s c) kh kw -> t s o (c kh kw)", o=P, c=K_PASS)
+    out_view = out.rearrange("n (t o) h w -> t o n (h w)", o=P)
+
+    units = [(s, t, kh) for s in range(PASSES) for t in range(O_TILES) for kh in range(KH)]
+    rounds = [units[first : first + UNITS] for first in range(0, len(units), UNITS)]
+
+    with ExitStack() as stack:
+        keep = stack.enter_context(tc.tile_pool(name="keep", bufs=1))
+        g_in = stack.enter_context(tc.tile_pool(name="g_in", bufs=O_TILES * AHEAD))
+        x_in = stack.enter_context(tc.tile_pool(name="x_in", bufs=AHEAD))
+        work = stack.enter_context(tc.tile_pool(name="work", bufs=2))
+        unit_psum = stack.enter_context(tc.psum_pool(name="unit_psum", bufs=UNITS))
+        sum_psum = stack.enter_context(tc.psum_pool(name="sum_psum", bufs=1))
+        stack.enter_context(tc.manual_schedule())
+
+        identity = keep.tile([P, P], F32)
+        make_identity(nc, identity[:])
+
+        x_codes = keep.tile([P, PASSES * X_WIDTH], U32, align_bytes=64)
+        x_scales = keep.tile([P, PASSES * X_WIDTH], U8, align_bytes=64)
+        x_scales_row1 = keep.tile([P, PASSES * PIXELS], U8, align_bytes=64)
+        nc.vector.memset(
+            x_codes[:].bitcast(I32).rearrange("p (s c) -> p s c", c=X_WIDTH)[:, :, PIXELS:], 0
+        )
+        nc.vector.memset(x_scales[:].bitcast(I32), 0)
+
+        sums = [
+            [sum_psum.tile([P, PIXELS], F32, name="sum_%d_%d" % (t, kw)) for kw in range(KW)]
+            for t in range(O_TILES)
+        ]
+
+        g_raw = {}
+        x_raw = {}
+
+        def load_g(s, t):
+            g_raw[(s, t)] = g_in.tile([P, K_PASS * KH * KW], BF16, name="g_raw")
+            nc.sync.dma_start(out=g_raw[(s, t)][:], in_=g_view[t, s])
+
+        def load_x(s):
+            x_raw[s] = x_in.tile([P, IMAGES, PACK * H * W], BF16, name="x_raw")
+            nc.sync.dma_start(out=x_raw[s][:], in_=x_view[s])
+
+        def transpose_unit(s, t, kh):
+            words = g_raw[(s, t)][:].bitcast(F32).rearrange(
+                "o (p j k) -> o j k p", j=PACK, k=KH
+            )
+            bank = unit_psum.tile([P, PACK * P], F32, name="bank")
+            for j in range(PACK):
+                nc.tensor.transpose(bank[:, j * P : (j + 1) * P], words[:, j, kh, :], identity[:])
+            return bank
+
+        def copy_unit_out(u, bank, g_grouped):
+            halves = bank[:].bitcast(BF16).rearrange("p (j o w) -> p w o j", j=PACK, w=KW)
+            grouped = g_grouped[:, u, :].rearrange("p (w o j) -> p w o j", w=KW, j=PACK)
+            if u < SCALAR_UNITS:
+                nc.scalar.copy(out=grouped, in_=halves)
+            else:
+                nc.vector.tensor_copy(out=grouped, in_=halves)
+
+        def quantise_round(g_grouped):
+            g_codes = work.tile([P, UNITS * KW * P], U32, align_bytes=64)
+            g_scales = work.tile([P, UNITS * KW * P], U8, align_bytes=64)
+            nc.vector.quantize_mx(
+                out=g_codes[:].bitcast(E5M2_X4),
+                scales=g_scales[:],
+                in_=g_grouped[:].rearrange("p u c -> p (u c)"),
+            )
+            return g_codes, g_scales
+
+        def multiply_round(round_units, g_codes, g_scales):
+            for u, (s, t, kh) in enumerate(round_units):
+                window = s * X_WIDTH + kh * ROW_STEP
+                if kh == 1:
+                    window_scales = x_scales_row1[:, s * PIXELS : (s + 1) * PIXELS]
+                else:
+                    window_scales = x_scales[:, window : window + PIXELS]
+                for kw in range(KW):
+                    o_cols = slice((u * KW + kw) * P, (u * KW + kw + 1) * P)
+                    nc.tensor.matmul_mx(
+                        out=sums[t][kw][:],
+                        lhsT=g_codes[:, o_cols].bitcast(E5M2_X4),
+                        lhsT_scale=g_scales[:, o_cols],
+                        rhs=x_codes[:, window : window + PIXELS].bitcast(E4M3_X4),
+                        rhs_scale=window_scales,
+                        start=(s == 0 and kh == 0),
+                        stop=(s == PASSES - 1 and kh == KH - 1),
+                    )
+
+        def group_x(s):
+            x_grouped = work.tile([P, PIXELS * PACK], BF16, align_bytes=64)
+            nc.vector.tensor_copy(
+                out=x_grouped[:].rearrange("p (h n w j) -> p h n w j", h=H, n=IMAGES, w=W),
+                in_=x_raw[s][:].rearrange("p n (j h w) -> p h n w j", j=PACK, w=W),
+            )
+            return x_grouped
+
+        def quantise_x(s, x_grouped):
+            first = s * X_WIDTH
+            nc.vector.quantize_mx(
+                out=x_codes[:, first : first + PIXELS].bitcast(E4M3_X4),
+                scales=x_scales[:, first : first + PIXELS],
+                in_=x_grouped[:],
+            )
+
+        def shift_x_scales(s):
+            first = s * X_WIDTH + ROW_STEP
+            nc.vector.tensor_copy(
+                out=x_scales_row1[:, s * PIXELS : (s + 1) * PIXELS].bitcast(I32),
+                in_=x_scales[:, first : first + PIXELS].bitcast(I32),
+            )
+
+        for s in range(AHEAD):
+            for t in range(O_TILES):
+                load_g(s, t)
+            load_x(s)
+
+        grouped_before = None
+        for r in range(len(rounds) + 1):
+            if r > 0:
+                g_codes, g_scales = quantise_round(grouped_before)
+            if r < len(rounds):
+                banks = [transpose_unit(s, t, kh) for (s, t, kh) in rounds[r]]
+            if r > 0:
+                multiply_round(rounds[r - 1], g_codes, g_scales)
+            if r == len(rounds):
+                break
+
+            for s, t, kh in rounds[r]:
+                if kh == KH - 1 and s + AHEAD < PASSES:
+                    load_g(s + AHEAD, t)
+
+            new_passes = [s for (s, t, kh) in rounds[r] if t == 0 and kh == 0]
+            g_grouped = work.tile([P, UNITS, KW * P * PACK], BF16, align_bytes=64)
+            for u in range(SCALAR_UNITS):
+                copy_unit_out(u, banks[u], g_grouped)
+            x_grouped = [group_x(s) for s in new_passes]
+            for s in new_passes:
+                if s + AHEAD < PASSES:
+                    load_x(s + AHEAD)
+            for u in range(SCALAR_UNITS, UNITS):
+                copy_unit_out(u, banks[u], g_grouped)
+            for s, grouped in zip(new_passes, x_grouped):
+                quantise_x(s, grouped)
+            for s in new_passes:
+                shift_x_scales(s)
+            grouped_before = g_grouped
+
+        for t in range(O_TILES):
+            by_pixel = [
+                sums[t][kw][:].rearrange("p (h n w) -> p n h w", n=IMAGES, w=W) for kw in range(KW)
+            ]
+            left = work.tile([P, IMAGES, HO, WO], F32)
+            nc.scalar.copy(out=left[:], in_=by_pixel[0][:, :, 0:HO, 0:WO])
+            total = work.tile([P, IMAGES, HO, WO], F32)
+            nc.vector.tensor_tensor(
+                out=total[:],
+                in0=by_pixel[1][:, :, 0:HO, 1 : WO + 1],
+                in1=left[:],
+                op=mybir.AluOpType.add,
+            )
+            nc.sync.dma_start(out=out_view[t], in_=total[:].rearrange("p n h w -> p n (h w)"))

@@ -25,7 +25,6 @@ PAD = (KH - 1) * ROW_STEP
 X_WIDTH = PIXELS + PAD
 
 UNITS = 4
-SCALAR_UNITS = 3
 AHEAD = 4
 
 FLOPS = 2 * CO * CI * KH * KW * IMAGES * HO * WO
@@ -39,7 +38,8 @@ def tile_model_pa_k_kernel(tc, x, grad_output, g, out):
     out_view = out.rearrange("n (t o) h w -> t o n (h w)", o=P)
 
     units = [(s, t, kh) for s in range(PASSES) for t in range(O_TILES) for kh in range(KH)]
-    rounds = [units[first : first + UNITS] for first in range(0, len(units), UNITS)]
+    firsts = [0] + list(range(UNITS // 2, len(units), UNITS))
+    rounds = [units[a:b] for a, b in zip(firsts, firsts[1:] + [len(units)])]
 
     with ExitStack() as stack:
         keep = stack.enter_context(tc.tile_pool(name="keep", bufs=1))
@@ -86,21 +86,19 @@ def tile_model_pa_k_kernel(tc, x, grad_output, g, out):
                 nc.tensor.transpose(bank[:, j * P : (j + 1) * P], words[:, j, kh, :], identity[:])
             return bank
 
-        def copy_unit_out(u, bank, g_grouped):
-            halves = bank[:].bitcast(BF16).rearrange("p (j o w) -> p w o j", j=PACK, w=KW)
-            grouped = g_grouped[:, u, :].rearrange("p (w o j) -> p w o j", w=KW, j=PACK)
-            if u < SCALAR_UNITS:
-                nc.scalar.copy(out=grouped, in_=halves)
-            else:
-                nc.vector.tensor_copy(out=grouped, in_=halves)
+        def copy_unit_out(copy, bank, grouped_unit):
+            copy(
+                out=grouped_unit.rearrange("p (w o j) -> p w o j", w=KW, j=PACK),
+                in_=bank[:].bitcast(BF16).rearrange("p (j o w) -> p w o j", j=PACK, w=KW),
+            )
 
-        def quantise_round(g_grouped):
+        def quantise_round(count, g_grouped):
             g_codes = work.tile([P, UNITS * KW * P], U32, align_bytes=64)
             g_scales = work.tile([P, UNITS * KW * P], U8, align_bytes=64)
             nc.vector.quantize_mx(
-                out=g_codes[:].bitcast(E5M2_X4),
-                scales=g_scales[:],
-                in_=g_grouped[:].rearrange("p u c -> p (u c)"),
+                out=g_codes[:, 0 : count * KW * P].bitcast(E5M2_X4),
+                scales=g_scales[:, 0 : count * KW * P],
+                in_=g_grouped[:, 0:count, :].rearrange("p u c -> p (u c)"),
             )
             return g_codes, g_scales
 
@@ -147,14 +145,18 @@ def tile_model_pa_k_kernel(tc, x, grad_output, g, out):
             )
 
         for s in range(AHEAD):
+            load_x(s)
             for t in range(O_TILES):
                 load_g(s, t)
-            load_x(s)
+
+        quantise_x(0, group_x(0))
+        shift_x_scales(0)
+        load_x(AHEAD)
 
         grouped_before = None
         for r in range(len(rounds) + 1):
             if r > 0:
-                g_codes, g_scales = quantise_round(grouped_before)
+                g_codes, g_scales = quantise_round(len(rounds[r - 1]), grouped_before)
             if r < len(rounds):
                 banks = [transpose_unit(s, t, kh) for (s, t, kh) in rounds[r]]
             if r > 0:
@@ -166,19 +168,18 @@ def tile_model_pa_k_kernel(tc, x, grad_output, g, out):
                 if kh == KH - 1 and s + AHEAD < PASSES:
                     load_g(s + AHEAD, t)
 
-            new_passes = [s for (s, t, kh) in rounds[r] if t == 0 and kh == 0]
+            new_passes = [s for (s, t, kh) in rounds[r] if t == 0 and kh == 0 and s > 0]
             g_grouped = work.tile([P, UNITS, KW * P * PACK], BF16, align_bytes=64)
-            for u in range(SCALAR_UNITS):
-                copy_unit_out(u, banks[u], g_grouped)
-            x_grouped = [group_x(s) for s in new_passes]
+            last = len(banks) - 1
+            for u in range(last):
+                copy_unit_out(nc.scalar.copy, banks[u], g_grouped[:, u, :])
+            new_grouped = [group_x(s) for s in new_passes]
             for s in new_passes:
                 if s + AHEAD < PASSES:
                     load_x(s + AHEAD)
-            for u in range(SCALAR_UNITS, UNITS):
-                copy_unit_out(u, banks[u], g_grouped)
-            for s, grouped in zip(new_passes, x_grouped):
-                quantise_x(s, grouped)
-            for s in new_passes:
+            copy_unit_out(nc.vector.tensor_copy, banks[last], g_grouped[:, last, :])
+            for s, x_grouped in zip(new_passes, new_grouped):
+                quantise_x(s, x_grouped)
                 shift_x_scales(s)
             grouped_before = g_grouped
 

@@ -26,6 +26,10 @@ X_WIDTH = PIXELS + PAD
 
 UNITS = 4
 AHEAD = 4
+LAG = 2
+SORT_AHEAD = 2
+SORT_BUFS = 6
+VECTOR_EVERY = 4
 
 FLOPS = 2 * CO * CI * KH * KW * IMAGES * HO * WO
 
@@ -45,6 +49,8 @@ def tile_model_pa_k_kernel(tc, x, grad_output, g, out):
         keep = stack.enter_context(tc.tile_pool(name="keep", bufs=1))
         g_in = stack.enter_context(tc.tile_pool(name="g_in", bufs=O_TILES * AHEAD))
         x_in = stack.enter_context(tc.tile_pool(name="x_in", bufs=AHEAD))
+        g_sort = stack.enter_context(tc.tile_pool(name="g_sort", bufs=SORT_BUFS))
+        stage = stack.enter_context(tc.tile_pool(name="stage", bufs=LAG + 1))
         work = stack.enter_context(tc.tile_pool(name="work", bufs=2))
         unit_psum = stack.enter_context(tc.psum_pool(name="unit_psum", bufs=UNITS))
         sum_psum = stack.enter_context(tc.psum_pool(name="sum_psum", bufs=1))
@@ -67,6 +73,7 @@ def tile_model_pa_k_kernel(tc, x, grad_output, g, out):
         ]
 
         g_raw = {}
+        g_sorted = {}
         x_raw = {}
 
         def load_g(s, t):
@@ -77,10 +84,15 @@ def tile_model_pa_k_kernel(tc, x, grad_output, g, out):
             x_raw[s] = x_in.tile([P, IMAGES, PACK * H * W], BF16, name="x_raw")
             nc.sync.dma_start(out=x_raw[s][:], in_=x_view[s])
 
-        def transpose_unit(s, t, kh):
-            words = g_raw[(s, t)][:].bitcast(F32).rearrange(
-                "o (p j k) -> o j k p", j=PACK, k=KH
+        def sort_tile(s, t):
+            g_sorted[(s, t)] = g_sort.tile([P, PACK * KH * P], F32, name="g_sorted")
+            nc.vector.tensor_copy(
+                out=g_sorted[(s, t)][:].rearrange("o (j k p) -> o j k p", j=PACK, k=KH),
+                in_=g_raw[(s, t)][:].bitcast(F32).rearrange("o (p j k) -> o j k p", j=PACK, k=KH),
             )
+
+        def transpose_unit(s, t, kh):
+            words = g_sorted[(s, t)][:].rearrange("o (j k p) -> o j k p", j=PACK, k=KH)
             bank = unit_psum.tile([P, PACK * P], F32, name="bank")
             for j in range(PACK):
                 nc.tensor.transpose(bank[:, j * P : (j + 1) * P], words[:, j, kh, :], identity[:])
@@ -93,8 +105,8 @@ def tile_model_pa_k_kernel(tc, x, grad_output, g, out):
             )
 
         def quantise_round(count, g_grouped):
-            g_codes = work.tile([P, UNITS * KW * P], U32, align_bytes=64)
-            g_scales = work.tile([P, UNITS * KW * P], U8, align_bytes=64)
+            g_codes = stage.tile([P, UNITS * KW * P], U32, align_bytes=64)
+            g_scales = stage.tile([P, UNITS * KW * P], U8, align_bytes=64)
             nc.vector.quantize_mx(
                 out=g_codes[:, 0 : count * KW * P].bitcast(E5M2_X4),
                 scales=g_scales[:, 0 : count * KW * P],
@@ -149,39 +161,54 @@ def tile_model_pa_k_kernel(tc, x, grad_output, g, out):
             for t in range(O_TILES):
                 load_g(s, t)
 
-        quantise_x(0, group_x(0))
+        tiles = [(s, t) for s in range(PASSES) for t in range(O_TILES)]
+        tiles_sorted = []
+
+        def sort_up_to(unit_count):
+            for s, t in tiles[len(tiles_sorted) :]:
+                if KH * len(tiles_sorted) >= unit_count:
+                    break
+                sort_tile(s, t)
+                tiles_sorted.append((s, t))
+                if s + AHEAD < PASSES:
+                    load_g(s + AHEAD, t)
+
+        ends = firsts[1:] + [len(units)]
+
+        x_grouped_0 = group_x(0)
+        sort_up_to(ends[SORT_AHEAD - 1])
+        quantise_x(0, x_grouped_0)
         shift_x_scales(0)
         load_x(AHEAD)
 
-        grouped_before = None
-        for r in range(len(rounds) + 1):
-            if r > 0:
-                g_codes, g_scales = quantise_round(len(rounds[r - 1]), grouped_before)
+        grouped = {}
+        codes = {}
+        for r in range(len(rounds) + LAG):
+            if 1 <= r <= len(rounds):
+                codes[r - 1] = quantise_round(len(rounds[r - 1]), grouped[r - 1])
             if r < len(rounds):
                 banks = [transpose_unit(s, t, kh) for (s, t, kh) in rounds[r]]
-            if r > 0:
-                multiply_round(rounds[r - 1], g_codes, g_scales)
-            if r == len(rounds):
-                break
+            if r >= LAG:
+                multiply_round(rounds[r - LAG], codes[r - LAG][0], codes[r - LAG][1])
+            if r < len(rounds):
+                g_grouped = stage.tile([P, UNITS, KW * P * PACK], BF16, align_bytes=64)
+                grouped[r] = g_grouped
+                last = len(banks) - 1
+                vector_helps = r % VECTOR_EVERY == VECTOR_EVERY - 1 or r == len(rounds) - 1
+                if vector_helps:
+                    copy_unit_out(nc.vector.tensor_copy, banks[last], g_grouped[:, last, :])
+                for u in range(last if vector_helps else last + 1):
+                    copy_unit_out(nc.scalar.copy, banks[u], g_grouped[:, u, :])
 
-            for s, t, kh in rounds[r]:
-                if kh == KH - 1 and s + AHEAD < PASSES:
-                    load_g(s + AHEAD, t)
-
-            new_passes = [s for (s, t, kh) in rounds[r] if t == 0 and kh == 0 and s > 0]
-            g_grouped = work.tile([P, UNITS, KW * P * PACK], BF16, align_bytes=64)
-            last = len(banks) - 1
-            for u in range(last):
-                copy_unit_out(nc.scalar.copy, banks[u], g_grouped[:, u, :])
-            new_grouped = [group_x(s) for s in new_passes]
-            for s in new_passes:
-                if s + AHEAD < PASSES:
-                    load_x(s + AHEAD)
-            copy_unit_out(nc.vector.tensor_copy, banks[last], g_grouped[:, last, :])
-            for s, x_grouped in zip(new_passes, new_grouped):
-                quantise_x(s, x_grouped)
-                shift_x_scales(s)
-            grouped_before = g_grouped
+                new_passes = [s for (s, t, kh) in rounds[r] if t == 0 and kh == 0 and s > 0]
+                new_grouped = [group_x(s) for s in new_passes]
+                for s in new_passes:
+                    if s + AHEAD < PASSES:
+                        load_x(s + AHEAD)
+                sort_up_to(ends[min(r + SORT_AHEAD, len(rounds) - 1)])
+                for s, x_grouped in zip(new_passes, new_grouped):
+                    quantise_x(s, x_grouped)
+                    shift_x_scales(s)
 
         for t in range(O_TILES):
             by_pixel = [

@@ -87,8 +87,8 @@ def tile_model_pa_k_kernel(tc, x, grad_output, g, out):
         def sort_tile(s, t):
             g_sorted[(s, t)] = g_sort.tile([P, PACK * KH * P], F32, name="g_sorted")
             nc.vector.tensor_copy(
-                out=g_sorted[(s, t)][:].rearrange("o (j k p) -> o j k p", j=PACK, k=KH),
-                in_=g_raw[(s, t)][:].bitcast(F32).rearrange("o (p j k) -> o j k p", j=PACK, k=KH),
+                out=g_sorted[(s, t)][:].rearrange("o (l i h p) -> o h l p i", l=KH, i=PACK, h=2),
+                in_=g_raw[(s, t)][:].bitcast(F32).rearrange("o (h p l i) -> o h l p i", l=KH, i=PACK, h=2),
             )
 
         def transpose_unit(s, t, kh):

@@ -28,8 +28,9 @@ UNITS = 4
 AHEAD = 4
 LAG = 2
 SORT_AHEAD = 2
-SORT_BUFS = 6
-VECTOR_EVERY = 4
+SORTED_T = (0,)
+SORT_BUFS = 4
+VECTOR_EVERY = 2
 
 FLOPS = 2 * CO * CI * KH * KW * IMAGES * HO * WO
 
@@ -47,7 +48,7 @@ def tile_model_pa_k_kernel(tc, x, grad_output, g, out):
 
     with ExitStack() as stack:
         keep = stack.enter_context(tc.tile_pool(name="keep", bufs=1))
-        g_in = stack.enter_context(tc.tile_pool(name="g_in", bufs=O_TILES * AHEAD))
+        g_in = stack.enter_context(tc.tile_pool(name="g_in", bufs=AHEAD))
         x_in = stack.enter_context(tc.tile_pool(name="x_in", bufs=AHEAD))
         g_sort = stack.enter_context(tc.tile_pool(name="g_sort", bufs=SORT_BUFS))
         stage = stack.enter_context(tc.tile_pool(name="stage", bufs=LAG + 1))
@@ -77,7 +78,7 @@ def tile_model_pa_k_kernel(tc, x, grad_output, g, out):
         x_raw = {}
 
         def load_g(s, t):
-            g_raw[(s, t)] = g_in.tile([P, K_PASS * KH * KW], BF16, name="g_raw")
+            g_raw[(s, t)] = g_in.tile([P, K_PASS * KH * KW], BF16, name="g_raw_%d" % t)
             nc.sync.dma_start(out=g_raw[(s, t)][:], in_=g_view[t, s])
 
         def load_x(s):
@@ -92,7 +93,10 @@ def tile_model_pa_k_kernel(tc, x, grad_output, g, out):
             )
 
         def transpose_unit(s, t, kh):
-            words = g_sorted[(s, t)][:].rearrange("o (j k p) -> o j k p", j=PACK, k=KH)
+            if t in SORTED_T:
+                words = g_sorted[(s, t)][:].rearrange("o (j k p) -> o j k p", j=PACK, k=KH)
+            else:
+                words = g_raw[(s, t)][:].bitcast(F32).rearrange("o (p j k) -> o j k p", j=PACK, k=KH)
             bank = unit_psum.tile([P, PACK * P], F32, name="bank")
             for j in range(PACK):
                 nc.tensor.transpose(bank[:, j * P : (j + 1) * P], words[:, j, kh, :], identity[:])
@@ -161,12 +165,12 @@ def tile_model_pa_k_kernel(tc, x, grad_output, g, out):
             for t in range(O_TILES):
                 load_g(s, t)
 
-        tiles = [(s, t) for s in range(PASSES) for t in range(O_TILES)]
+        tiles = [(s, t) for s in range(PASSES) for t in range(O_TILES) if t in SORTED_T]
         tiles_sorted = []
 
         def sort_up_to(unit_count):
             for s, t in tiles[len(tiles_sorted) :]:
-                if KH * len(tiles_sorted) >= unit_count:
+                if units.index((s, t, 0)) >= unit_count:
                     break
                 sort_tile(s, t)
                 tiles_sorted.append((s, t))
@@ -191,6 +195,10 @@ def tile_model_pa_k_kernel(tc, x, grad_output, g, out):
             if r >= LAG:
                 multiply_round(rounds[r - LAG], codes[r - LAG][0], codes[r - LAG][1])
             if r < len(rounds):
+                for s, t, kh in rounds[r]:
+                    if t not in SORTED_T and kh == KH - 1 and s + AHEAD < PASSES:
+                        load_g(s + AHEAD, t)
+
                 g_grouped = stage.tile([P, UNITS, KW * P * PACK], BF16, align_bytes=64)
                 grouped[r] = g_grouped
                 last = len(banks) - 1

@@ -187,9 +187,14 @@ def tile_model_pa_k_kernel(tc, x, grad_output, g, out):
 
         grouped = {}
         codes = {}
+        x_waiting = []
         for r in range(len(rounds) + LAG):
             if 1 <= r <= len(rounds):
                 codes[r - 1] = quantise_round(len(rounds[r - 1]), grouped[r - 1])
+            x_quantised = [s for s, x_grouped in x_waiting]
+            for s, x_grouped in x_waiting:
+                quantise_x(s, x_grouped)
+            x_waiting = []
             if r < len(rounds):
                 banks = [transpose_unit(s, t, kh) for (s, t, kh) in rounds[r]]
             if r >= LAG:
@@ -208,15 +213,13 @@ def tile_model_pa_k_kernel(tc, x, grad_output, g, out):
                 for u in range(last if vector_helps else last + 1):
                     copy_unit_out(nc.scalar.copy, banks[u], g_grouped[:, u, :])
 
-                new_passes = [s for (s, t, kh) in rounds[r] if t == 0 and kh == 0 and s > 0]
-                new_grouped = [group_x(s) for s in new_passes]
-                for s in new_passes:
+                for s in [s for (s, t, kh) in rounds[r] if t == 0 and kh == 0 and s > 0]:
+                    x_waiting.append((s, group_x(s)))
                     if s + AHEAD < PASSES:
                         load_x(s + AHEAD)
                 sort_up_to(ends[min(r + SORT_AHEAD, len(rounds) - 1)])
-                for s, x_grouped in zip(new_passes, new_grouped):
-                    quantise_x(s, x_grouped)
-                    shift_x_scales(s)
+            for s in x_quantised:
+                shift_x_scales(s)
 
         for t in range(O_TILES):
             by_pixel = [

@@ -28,7 +28,7 @@ UNITS = 4
 AHEAD = 4
 LAG = 2
 SORT_AHEAD = 2
-SORTED_T = (0,)
+HEAD_ROUNDS = 5
 SORT_BUFS = 4
 VECTOR_EVERY = 2
 
@@ -43,8 +43,14 @@ def tile_model_pa_k_kernel(tc, x, grad_output, g, out):
     out_view = out.rearrange("n (t o) h w -> t o n (h w)", o=P)
 
     units = [(s, t, kh) for s in range(PASSES) for t in range(O_TILES) for kh in range(KH)]
-    firsts = [0] + list(range(UNITS // 2, len(units), UNITS))
+    short = UNITS // 2
+    sizes = [short] * HEAD_ROUNDS
+    sizes = sizes + [UNITS] * ((len(units) - sum(sizes) - short) // UNITS) + [short]
+    firsts = [sum(sizes[:r]) for r in range(len(sizes))]
     rounds = [units[a:b] for a, b in zip(firsts, firsts[1:] + [len(units)])]
+
+    def is_sorted(s, t):
+        return t == 0 and s > 0
 
     with ExitStack() as stack:
         keep = stack.enter_context(tc.tile_pool(name="keep", bufs=1))
@@ -93,7 +99,7 @@ def tile_model_pa_k_kernel(tc, x, grad_output, g, out):
             )
 
         def transpose_unit(s, t, kh):
-            if t in SORTED_T:
+            if is_sorted(s, t):
                 words = g_sorted[(s, t)][:].rearrange("o (j k p) -> o j k p", j=PACK, k=KH)
             else:
                 words = g_raw[(s, t)][:].bitcast(F32).rearrange("o (p j k) -> o j k p", j=PACK, k=KH)
@@ -161,11 +167,11 @@ def tile_model_pa_k_kernel(tc, x, grad_output, g, out):
             )
 
         for s in range(AHEAD):
+            load_g(s, 0)
             load_x(s)
-            for t in range(O_TILES):
-                load_g(s, t)
+            load_g(s, 1)
 
-        tiles = [(s, t) for s in range(PASSES) for t in range(O_TILES) if t in SORTED_T]
+        tiles = [(s, t) for s in range(PASSES) for t in range(O_TILES) if is_sorted(s, t)]
         tiles_sorted = []
 
         def sort_up_to(unit_count):
@@ -201,7 +207,7 @@ def tile_model_pa_k_kernel(tc, x, grad_output, g, out):
                 multiply_round(rounds[r - LAG], codes[r - LAG][0], codes[r - LAG][1])
             if r < len(rounds):
                 for s, t, kh in rounds[r]:
-                    if t not in SORTED_T and kh == KH - 1 and s + AHEAD < PASSES:
+                    if not is_sorted(s, t) and kh == KH - 1 and s + AHEAD < PASSES:
                         load_g(s + AHEAD, t)
 
                 g_grouped = stage.tile([P, UNITS, KW * P * PACK], BF16, align_bytes=64)

@@ -24,13 +24,13 @@ ROW_STEP = IMAGES * W
 PAD = (KH - 1) * ROW_STEP
 X_WIDTH = PIXELS + PAD
 
-UNITS = 4
+UNITS = KH
+BANKS = 4
 AHEAD = 4
 LAG = 2
 SORT_AHEAD = 2
-HEAD_ROUNDS = 5
 SORT_BUFS = 4
-VECTOR_EVERY = 2
+VECTOR_EVERY = 3
 
 FLOPS = 2 * CO * CI * KH * KW * IMAGES * HO * WO
 
@@ -43,14 +43,12 @@ def tile_model_pa_k_kernel(tc, x, grad_output, g, out):
     out_view = out.rearrange("n (t o) h w -> t o n (h w)", o=P)
 
     units = [(s, t, kh) for s in range(PASSES) for t in range(O_TILES) for kh in range(KH)]
-    short = UNITS // 2
-    sizes = [short] * HEAD_ROUNDS
-    sizes = sizes + [UNITS] * ((len(units) - sum(sizes) - short) // UNITS) + [short]
+    sizes = [1, UNITS - 1] + [UNITS] * (len(units) // UNITS - 1)
     firsts = [sum(sizes[:r]) for r in range(len(sizes))]
     rounds = [units[a:b] for a, b in zip(firsts, firsts[1:] + [len(units)])]
 
     def is_sorted(s, t):
-        return t == 0 and s > 0
+        return s > 0 and (t == 0 or s % 2 == 1)
 
     with ExitStack() as stack:
         keep = stack.enter_context(tc.tile_pool(name="keep", bufs=1))
@@ -59,7 +57,7 @@ def tile_model_pa_k_kernel(tc, x, grad_output, g, out):
         g_sort = stack.enter_context(tc.tile_pool(name="g_sort", bufs=SORT_BUFS))
         stage = stack.enter_context(tc.tile_pool(name="stage", bufs=LAG + 1))
         work = stack.enter_context(tc.tile_pool(name="work", bufs=2))
-        unit_psum = stack.enter_context(tc.psum_pool(name="unit_psum", bufs=UNITS))
+        unit_psum = stack.enter_context(tc.psum_pool(name="unit_psum", bufs=BANKS))
         sum_psum = stack.enter_context(tc.psum_pool(name="sum_psum", bufs=1))
         stack.enter_context(tc.manual_schedule())
 
@@ -117,11 +115,13 @@ def tile_model_pa_k_kernel(tc, x, grad_output, g, out):
         def quantise_round(count, g_grouped):
             g_codes = stage.tile([P, UNITS * KW * P], U32, align_bytes=64)
             g_scales = stage.tile([P, UNITS * KW * P], U8, align_bytes=64)
-            nc.vector.quantize_mx(
-                out=g_codes[:, 0 : count * KW * P].bitcast(E5M2_X4),
-                scales=g_scales[:, 0 : count * KW * P],
-                in_=g_grouped[:, 0:count, :].rearrange("p u c -> p (u c)"),
-            )
+            for first in range(0, count, 2):
+                behind = min(first + 2, count)
+                nc.vector.quantize_mx(
+                    out=g_codes[:, first * KW * P : behind * KW * P].bitcast(E5M2_X4),
+                    scales=g_scales[:, first * KW * P : behind * KW * P],
+                    in_=g_grouped[:, first:behind, :].rearrange("p u c -> p (u c)"),
+                )
             return g_codes, g_scales
 
         def multiply_round(round_units, g_codes, g_scales):
@@ -166,6 +166,15 @@ def tile_model_pa_k_kernel(tc, x, grad_output, g, out):
                 in_=x_scales[:, first : first + PIXELS].bitcast(I32),
             )
 
+        released = set()
+        next_load = [AHEAD for t in range(O_TILES)]
+
+        def release(s, t):
+            released.add((s, t))
+            while next_load[t] < PASSES and (next_load[t] - AHEAD, t) in released:
+                load_g(next_load[t], t)
+                next_load[t] += 1
+
         for s in range(AHEAD):
             load_g(s, 0)
             load_x(s)
@@ -180,8 +189,7 @@ def tile_model_pa_k_kernel(tc, x, grad_output, g, out):
                     break
                 sort_tile(s, t)
                 tiles_sorted.append((s, t))
-                if s + AHEAD < PASSES:
-                    load_g(s + AHEAD, t)
+                release(s, t)
 
         ends = firsts[1:] + [len(units)]
 
@@ -207,8 +215,8 @@ def tile_model_pa_k_kernel(tc, x, grad_output, g, out):
                 multiply_round(rounds[r - LAG], codes[r - LAG][0], codes[r - LAG][1])
             if r < len(rounds):
                 for s, t, kh in rounds[r]:
-                    if not is_sorted(s, t) and kh == KH - 1 and s + AHEAD < PASSES:
-                        load_g(s + AHEAD, t)
+                    if not is_sorted(s, t) and kh == KH - 1:
+                        release(s, t)
 
                 g_grouped = stage.tile([P, UNITS, KW * P * PACK], BF16, align_bytes=64)
                 grouped[r] = g_grouped
@@ -219,11 +227,11 @@ def tile_model_pa_k_kernel(tc, x, grad_output, g, out):
                 for u in range(last if vector_helps else last + 1):
                     copy_unit_out(nc.scalar.copy, banks[u], g_grouped[:, u, :])
 
-                for s in [s for (s, t, kh) in rounds[r] if t == 0 and kh == 0 and s > 0]:
+                sort_up_to(ends[min(r + SORT_AHEAD, len(rounds) - 1)])
+                for s in [s for (s, t, kh) in rounds[min(r + 1, len(rounds) - 1)] if t == 0 and kh == 0 and s > 0]:
                     x_waiting.append((s, group_x(s)))
                     if s + AHEAD < PASSES:
                         load_x(s + AHEAD)
-                sort_up_to(ends[min(r + SORT_AHEAD, len(rounds) - 1)])
             for s in x_quantised:
                 shift_x_scales(s)
 

from contextlib import ExitStack

import concourse.mybir as mybir
from concourse.masks import make_identity

BF16 = mybir.dt.bfloat16
F32 = mybir.dt.float32
I32 = mybir.dt.int32
U32 = mybir.dt.uint32
U8 = mybir.dt.uint8
E4M3_X4 = mybir.dt.float8_e4m3fn_x4
E5M2_X4 = mybir.dt.float8_e5m2_x4

IMAGES, CI, CO, H, W, KH, KW = 2, 8192, 256, 16, 16, 3, 2
HO, WO = H - KH + 1, W - KW + 1

P = 128
PACK = 4
K_PASS = P * PACK
PASSES = CI // K_PASS
O_TILES = CO // P
PIXELS = IMAGES * H * W
ROW_STEP = IMAGES * W
PAD = (KH - 1) * ROW_STEP
X_WIDTH = PIXELS + PAD

UNITS = KH
BANKS = 4
AHEAD = 4
LAG = 2
SORT_AHEAD = 2
SORT_BUFS = 4
VECTOR_EVERY = 3

FLOPS = 2 * CO * CI * KH * KW * IMAGES * HO * WO


def tile_model_pa_k_kernel(tc, x, grad_output, g, out):
    nc = tc.nc

    x_view = x.rearrange("n (s p j) h w -> s p n (j h w)", p=P, j=PACK)
    g_view = g.rearrange("(t o) (s c) kh kw -> t s o (c kh kw)", o=P, c=K_PASS)
    out_view = out.rearrange("n (t o) h w -> t o n (h w)", o=P)

    units = [(s, t, kh) for s in range(PASSES) for t in range(O_TILES) for kh in range(KH)]
    sizes = [1, UNITS - 1] + [UNITS] * (len(units) // UNITS - 1)
    firsts = [sum(sizes[:r]) for r in range(len(sizes))]
    rounds = [units[a:b] for a, b in zip(firsts, firsts[1:] + [len(units)])]

    def is_sorted(s, t):
        return s > 0 and (t == 0 or s % 2 == 1)

    with ExitStack() as stack:
        keep = stack.enter_context(tc.tile_pool(name="keep", bufs=1))
        g_in = stack.enter_context(tc.tile_pool(name="g_in", bufs=AHEAD))
        x_in = stack.enter_context(tc.tile_pool(name="x_in", bufs=AHEAD))
        g_sort = stack.enter_context(tc.tile_pool(name="g_sort", bufs=SORT_BUFS))
        stage = stack.enter_context(tc.tile_pool(name="stage", bufs=LAG + 1))
        work = stack.enter_context(tc.tile_pool(name="work", bufs=2))
        unit_psum = stack.enter_context(tc.psum_pool(name="unit_psum", bufs=BANKS))
        sum_psum = stack.enter_context(tc.psum_pool(name="sum_psum", bufs=1))
        stack.enter_context(tc.manual_schedule())

        identity = keep.tile([P, P], F32)
        make_identity(nc, identity[:])

        x_codes = keep.tile([P, PASSES * X_WIDTH], U32, align_bytes=64)
        x_scales = keep.tile([P, PASSES * X_WIDTH], U8, align_bytes=64)
        x_scales_row1 = keep.tile([P, PASSES * PIXELS], U8, align_bytes=64)
        nc.vector.memset(
            x_codes[:].bitcast(I32).rearrange("p (s c) -> p s c", c=X_WIDTH)[:, :, PIXELS:], 0
        )
        nc.vector.memset(x_scales[:].bitcast(I32), 0)

        sums = [
            [sum_psum.tile([P, PIXELS], F32, name="sum_%d_%d" % (t, kw)) for kw in range(KW)]
            for t in range(O_TILES)
        ]

        g_raw = {}
        g_sorted = {}
        x_raw = {}

        def load_g(s, t):
            g_raw[(s, t)] = g_in.tile([P, K_PASS * KH * KW], BF16, name="g_raw_%d" % t)
            nc.sync.dma_start(out=g_raw[(s, t)][:], in_=g_view[t, s])

        def load_x(s):
            x_raw[s] = x_in.tile([P, IMAGES, PACK * H * W], BF16, name="x_raw")
            nc.sync.dma_start(out=x_raw[s][:], in_=x_view[s])

        def sort_tile(s, t):
            g_sorted[(s, t)] = g_sort.tile([P, PACK * KH * P], F32, name="g_sorted")
            nc.vector.tensor_copy(
                out=g_sorted[(s, t)][:].rearrange("o (l i h p) -> o h l p i", l=KH, i=PACK, h=2),
                in_=g_raw[(s, t)][:].bitcast(F32).rearrange("o (h p l i) -> o h l p i", l=KH, i=PACK, h=2),
            )

        def transpose_unit(s, t, kh):
            if is_sorted(s, t):
                words = g_sorted[(s, t)][:].rearrange("o (j k p) -> o j k p", j=PACK, k=KH)
            else:
                words = g_raw[(s, t)][:].bitcast(F32).rearrange("o (p j k) -> o j k p", j=PACK, k=KH)
            bank = unit_psum.tile([P, PACK * P], F32, name="bank")
            for j in range(PACK):
                nc.tensor.transpose(bank[:, j * P : (j + 1) * P], words[:, j, kh, :], identity[:])
            return bank

        def copy_unit_out(copy, bank, grouped_unit):
            copy(
                out=grouped_unit.rearrange("p (w o j) -> p w o j", w=KW, j=PACK),
                in_=bank[:].bitcast(BF16).rearrange("p (j o w) -> p w o j", j=PACK, w=KW),
            )

        def quantise_round(count, g_grouped):
            g_codes = stage.tile([P, UNITS * KW * P], U32, align_bytes=64)
            g_scales = stage.tile([P, UNITS * KW * P], U8, align_bytes=64)
            for first in range(0, count, 2):
                behind = min(first + 2, count)
                nc.vector.quantize_mx(
                    out=g_codes[:, first * KW * P : behind * KW * P].bitcast(E5M2_X4),
                    scales=g_scales[:, first * KW * P : behind * KW * P],
                    in_=g_grouped[:, first:behind, :].rearrange("p u c -> p (u c)"),
                )
            return g_codes, g_scales

        def multiply_round(round_units, g_codes, g_scales):
            for u, (s, t, kh) in enumerate(round_units):
                window = s * X_WIDTH + kh * ROW_STEP
                if kh == 1:
                    window_scales = x_scales_row1[:, s * PIXELS : (s + 1) * PIXELS]
                else:
                    window_scales = x_scales[:, window : window + PIXELS]
                for kw in range(KW):
                    o_cols = slice((u * KW + kw) * P, (u * KW + kw + 1) * P)
                    nc.tensor.matmul_mx(
                        out=sums[t][kw][:],
                        lhsT=g_codes[:, o_cols].bitcast(E5M2_X4),
                        lhsT_scale=g_scales[:, o_cols],
                        rhs=x_codes[:, window : window + PIXELS].bitcast(E4M3_X4),
                        rhs_scale=window_scales,
                        start=(s == 0 and kh == 0),
                        stop=(s == PASSES - 1 and kh == KH - 1),
                    )

        def group_x(s):
            x_grouped = work.tile([P, PIXELS * PACK], BF16, align_bytes=64)
            nc.vector.tensor_copy(
                out=x_grouped[:].rearrange("p (h n w j) -> p h n w j", h=H, n=IMAGES, w=W),
                in_=x_raw[s][:].rearrange("p n (j h w) -> p h n w j", j=PACK, w=W),
            )
            return x_grouped

        def quantise_x(s, x_grouped):
            first = s * X_WIDTH
            nc.vector.quantize_mx(
                out=x_codes[:, first : first + PIXELS].bitcast(E4M3_X4),
                scales=x_scales[:, first : first + PIXELS],
                in_=x_grouped[:],
            )

        def shift_x_scales(s):
            first = s * X_WIDTH + ROW_STEP
            nc.vector.tensor_copy(
                out=x_scales_row1[:, s * PIXELS : (s + 1) * PIXELS].bitcast(I32),
                in_=x_scales[:, first : first + PIXELS].bitcast(I32),
            )

        released = set()
        next_load = [AHEAD for t in range(O_TILES)]

        def release(s, t):
            released.add((s, t))
            while next_load[t] < PASSES and (next_load[t] - AHEAD, t) in released:
                load_g(next_load[t], t)
                next_load[t] += 1

        for s in range(AHEAD):
            load_g(s, 0)
            load_x(s)
            load_g(s, 1)

        tiles = [(s, t) for s in range(PASSES) for t in range(O_TILES) if is_sorted(s, t)]
        tiles_sorted = []

        def sort_up_to(unit_count):
            for s, t in tiles[len(tiles_sorted) :]:
                if units.index((s, t, 0)) >= unit_count:
                    break
                sort_tile(s, t)
                tiles_sorted.append((s, t))
                release(s, t)

        ends = firsts[1:] + [len(units)]

        x_grouped_0 = group_x(0)
        sort_up_to(ends[SORT_AHEAD - 1])
        quantise_x(0, x_grouped_0)
        shift_x_scales(0)
        load_x(AHEAD)

        grouped = {}
        codes = {}
        x_waiting = []
        for r in range(len(rounds) + LAG):
            if 1 <= r <= len(rounds):
                codes[r - 1] = quantise_round(len(rounds[r - 1]), grouped[r - 1])
            x_quantised = [s for s, x_grouped in x_waiting]
            for s, x_grouped in x_waiting:
                quantise_x(s, x_grouped)
            x_waiting = []
            if r < len(rounds):
                banks = [transpose_unit(s, t, kh) for (s, t, kh) in rounds[r]]
            if r >= LAG:
                multiply_round(rounds[r - LAG], codes[r - LAG][0], codes[r - LAG][1])
            if r < len(rounds):
                for s, t, kh in rounds[r]:
                    if not is_sorted(s, t) and kh == KH - 1:
                        release(s, t)

                g_grouped = stage.tile([P, UNITS, KW * P * PACK], BF16, align_bytes=64)
                grouped[r] = g_grouped
                last = len(banks) - 1
                vector_helps = r % VECTOR_EVERY == VECTOR_EVERY - 1 or r == len(rounds) - 1
                if vector_helps:
                    copy_unit_out(nc.vector.tensor_copy, banks[last], g_grouped[:, last, :])
                for u in range(last if vector_helps else last + 1):
                    copy_unit_out(nc.scalar.copy, banks[u], g_grouped[:, u, :])

                sort_up_to(ends[min(r + SORT_AHEAD, len(rounds) - 1)])
                for s in [s for (s, t, kh) in rounds[min(r + 1, len(rounds) - 1)] if t == 0 and kh == 0 and s > 0]:
                    x_waiting.append((s, group_x(s)))
                    if s + AHEAD < PASSES:
                        load_x(s + AHEAD)
            for s in x_quantised:
                shift_x_scales(s)

        for t in range(O_TILES):
            by_pixel = [
                sums[t][kw][:].rearrange("p (h n w) -> p n h w", n=IMAGES, w=W) for kw in range(KW)
            ]
            left = work.tile([P, IMAGES, HO, WO], F32)
            nc.scalar.copy(out=left[:], in_=by_pixel[0][:, :, 0:HO, 0:WO])
            total = work.tile([P, IMAGES, HO, WO], F32)
            nc.vector.tensor_tensor(
                out=total[:],
                in0=by_pixel[1][:, :, 0:HO, 1 : WO + 1],
                in1=left[:],
                op=mybir.AluOpType.add,
            )
            nc.sync.dma_start(out=out_view[t], in_=total[:].rearrange("p n h w -> p n (h w)"))
